import numpy as np
import ml_dtypes


def mxq(x, axis, fmt="e4m3"):
    dtype, down = {"e4m3": (ml_dtypes.float8_e4m3fn, 7), "e5m2": (ml_dtypes.float8_e5m2, 14)}[fmt]
    v = np.moveaxis(np.asarray(x, np.float32).astype(ml_dtypes.bfloat16).astype(np.float64), axis, -1)
    blocks = v.reshape(v.shape[:-1] + (-1, 32))
    amax = np.abs(blocks).max(-1, keepdims=True)
    byte = np.maximum(np.where(amax > 0, np.frexp(amax)[1] - 1 + 127, 0) - down, 1)
    scale = np.exp2(byte - 127.0)
    codes = (blocks / scale).astype(np.float32).astype(dtype).astype(np.float64)
    return np.moveaxis((codes * scale).reshape(v.shape), -1, axis)


WIDE = False


def mx_kscale(k):
    if not WIDE:
        return np.ones(k)
    levels = np.array([10, -10, 5, -5, 0])
    a = np.random.permutation(np.resize(levels, k // 512 * 4)).reshape(k // 512, 4)
    idx = np.arange(k)
    return np.exp2(a[idx // 512, idx % 128 // 32])


BF16 = ml_dtypes.bfloat16


def bf(x):
    return np.asarray(x, np.float32).astype(BF16)


def f64(x):
    return np.asarray(x).astype(np.float64)


E2M1 = np.array([0.0, 0.5, 1.0, 1.5, 2.0, 3.0, 4.0, 6.0, -0.0, -0.5, -1.0, -1.5, -2.0, -3.0, -4.0, -6.0])


def pack_weight(w, fmt):
    k, n = w.shape
    w = f64(bf(w)).reshape(k // 32, 32, n)
    amax = np.abs(w).max(1)
    if fmt == "e4m3":
        byte = np.frexp(amax)[1] - 1 + 127 - 7
    else:
        mant, ex = np.frexp(amax / 6.0)
        byte = np.where(mant > 0.5, ex, ex - 1) + 127
    byte = np.clip(np.where(amax > 0, byte, 1), 1, 254)
    scaled = (w * np.exp2(127.0 - byte)[:, None, :]).reshape(k, n).astype(np.float32)
    by_word = np.ascontiguousarray(scaled.reshape(k // 512, 128, 4, n).transpose(0, 1, 3, 2))
    if fmt == "e4m3":
        words = by_word.astype(ml_dtypes.float8_e4m3fn).view(np.uint8)
    else:
        c = by_word.astype(ml_dtypes.float4_e2m1fn).view(np.uint8) & 0xF
        words = c[..., 0::2] | (c[..., 1::2] << 4)
    return np.ascontiguousarray(words), np.ascontiguousarray(byte.astype(np.uint8).reshape(k // 512, 16, n))


def unpack_weight(words, scales, fmt):
    g, p, n, _ = words.shape
    if fmt == "e4m3":
        vals = np.ascontiguousarray(words).view(ml_dtypes.float8_e4m3fn).astype(np.float64)
    else:
        nib = np.empty((g, p, n, 4), np.uint8)
        nib[..., 0::2] = words & 0xF
        nib[..., 1::2] = words >> 4
        vals = E2M1[nib]
    vals = vals * np.repeat(np.exp2(scales.astype(np.float64) - 127.0), 8, axis=1)[..., None]
    return vals.transpose(0, 1, 3, 2).reshape(g * 512, n)


B, C, CQ, CV, H, W = 2, 8192, 128, 256, 16, 32
P = H * W
FMT = "e4m3"


def conv1x1(xq, w_words, w_scales, b):
    wt = unpack_weight(w_words, w_scales, FMT)
    y = (wt.T @ xq) + f64(b)[None, :, None]
    return y.reshape(B, wt.shape[1], H, W)


def kronecker(y):
    return np.concatenate([y.mean(axis=3), y.mean(axis=2)], axis=2)


def setup_inputs():
    s = mx_kscale(C)
    g = 3.0 / np.sqrt(C)
    x = bf(np.random.standard_normal((B, C, H, W)) * s[None, :, None, None])
    Wq_words, Wq_scales = pack_weight(np.ascontiguousarray((np.random.standard_normal((CQ, C)) * g / s[None, :]).T), FMT)
    bq = bf(np.random.standard_normal(CQ) * 0.1)
    Wk_words, Wk_scales = pack_weight(np.ascontiguousarray((np.random.standard_normal((CQ, C)) * g / s[None, :]).T), FMT)
    bk = bf(np.random.standard_normal(CQ) * 0.1)
    Wv_words, Wv_scales = pack_weight(np.ascontiguousarray((np.random.standard_normal((CV, C)) * g / s[None, :]).T), FMT)
    bv = bf(np.random.standard_normal(CV) * 0.1)
    return {"x": x,
            "Wq_words": Wq_words, "Wq_scales": Wq_scales,
            "bq": bq,
            "Wk_words": Wk_words, "Wk_scales": Wk_scales,
            "bk": bk,
            "Wv_words": Wv_words, "Wv_scales": Wv_scales,
            "bv": bv}


def reference(x, Wq_words, Wq_scales, bq, Wk_words, Wk_scales, bk, Wv_words, Wv_scales, bv):
    xq = mxq(f64(x).reshape(B, C, P), 1, "e4m3")
    q = kronecker(conv1x1(xq, Wq_words, Wq_scales, bq))
    k = kronecker(conv1x1(xq, Wk_words, Wk_scales, bk))
    v = kronecker(conv1x1(xq, Wv_words, Wv_scales, bv))
    return q, k, v

@@ -1,0 +1,186 @@
+from contextlib import ExitStack
+
+import concourse.mybir as mybir
+
+F32 = mybir.dt.float32
+BF16 = mybir.dt.bfloat16
+I32 = mybir.dt.int32
+U32 = mybir.dt.uint32
+U8 = mybir.dt.uint8
+FP8X4 = mybir.dt.float8_e4m3fn_x4
+ADD = mybir.AluOpType.add
+AXIS_X = mybir.AxisListType.X
+IDENTITY = mybir.ActivationFunctionType.Identity
+
+P = 128
+PACK = 4
+K_PASS = P * PACK
+
+IMAGES = 2
+CHANNELS = 8192
+ROWS = 16
+COLS = 32
+PIXELS = ROWS * COLS
+GROUPS = CHANNELS // K_PASS
+OUT_CHANNELS = 512
+O_TILES = OUT_CHANNELS // P
+POOLED = ROWS + COLS
+
+CHUNKS = IMAGES * GROUPS
+WEIGHT_GROUPS = 4
+WEIGHT_LEAD = 2
+RUN = 4
+VECTOR_PIXELS = 208
+
+FLOPS = 2 * IMAGES * PIXELS * CHANNELS * OUT_CHANNELS
+
+
+def tile_pam_module_pa_k_kernel(
+    tc, x, Wq_words, Wq_scales, bq, Wk_words, Wk_scales, bk, Wv_words, Wv_scales, bv, out_0, out_1, out_2
+):
+    nc = tc.nc
+    weights = [(Wq_words, Wq_scales, 0), (Wk_words, Wk_scales, P), (Wv_words, Wv_scales, 2 * P)]
+    bias_rows = [bq, bk, bv[0:P], bv[P : 2 * P]]
+    out_rows = [out_0, out_1, out_2[:, 0:P, :], out_2[:, P : 2 * P, :]]
+
+    with ExitStack() as stack:
+        keep = stack.enter_context(tc.tile_pool(name="keep", bufs=1))
+        raw_pool = stack.enter_context(tc.tile_pool(name="raw", bufs=8))
+        grouped_pool = stack.enter_context(tc.tile_pool(name="grouped", bufs=3))
+        quantised_pool = stack.enter_context(tc.tile_pool(name="quantised", bufs=6))
+        psum = stack.enter_context(tc.psum_pool(name="psum", bufs=1))
+        stack.enter_context(tc.manual_schedule())
+
+        w_words = keep.tile([P, GROUPS, OUT_CHANNELS], U32, align_bytes=64)
+        w_scales = keep.tile([P, GROUPS, OUT_CHANNELS], U8, align_bytes=64)
+        bias_bf16 = keep.tile([P, O_TILES, 16], BF16)
+        bias = keep.tile([P, O_TILES], F32)
+        pooled = keep.tile([P, IMAGES, O_TILES, POOLED], F32)
+        means = keep.tile([P, IMAGES, O_TILES, POOLED], F32)
+        sums_of = {}
+        for image in range(IMAGES):
+            for o_tile in range(O_TILES):
+                sums_of[(image, o_tile)] = psum.tile([P, PIXELS], F32, name="y_%d_%d" % (image, o_tile))
+
+        nc.vector.memset(w_scales[:].rearrange("p g n -> p (g n)").bitcast(I32), 0)
+
+        with nc.allow_non_contiguous_dma(reason="128 bias values, one to a partition"):
+            for o_tile in range(O_TILES):
+                nc.scalar.dma_start(
+                    out=bias_bf16[:, o_tile, 0:1], in_=bias_rows[o_tile].rearrange("(o u) -> o u", u=1)
+                )
+        nc.scalar.activation(out=bias[:], in_=bias_bf16[:, :, 0], func=IDENTITY)
+
+        def load_weight_scales():
+            for words, scales, first in weights:
+                n = scales.shape[2]
+                for quadrant in range(4):
+                    nc.sync.dma_start(
+                        out=w_scales[32 * quadrant : 32 * quadrant + 4, :, first : first + n].bitcast(I32),
+                        in_=scales[:, 4 * quadrant : 4 * quadrant + 4, :].rearrange("g q n -> q g n").bitcast(I32),
+                    )
+
+        def load_weight_words(first_group):
+            groups = slice(first_group, first_group + WEIGHT_GROUPS)
+            for words, scales, first in weights:
+                n = words.shape[2]
+                nc.sync.dma_start(
+                    out=w_words[:, groups, first : first + n].bitcast(I32),
+                    in_=words[groups].rearrange("g p n t -> p g (n t)").bitcast(I32),
+                )
+
+        def load_x(image, group):
+            raw = raw_pool.tile([P, PACK, PIXELS], BF16)
+            nc.sync.dma_start(
+                out=raw[:],
+                in_=x[image, group * K_PASS : (group + 1) * K_PASS].rearrange("(p t) h w -> p t (h w)", t=PACK),
+            )
+            return raw
+
+        def regroup(raw):
+            grouped = grouped_pool.tile([P, PIXELS, PACK], BF16, align_bytes=64)
+            for copy, pixels in (
+                (nc.vector.tensor_copy, slice(0, VECTOR_PIXELS)),
+                (nc.scalar.copy, slice(VECTOR_PIXELS, PIXELS)),
+            ):
+                copy(
+                    out=grouped[:, pixels, :].rearrange("p (c i) t -> p c t i", i=RUN),
+                    in_=raw[:, :, pixels].rearrange("p t (c i) -> p c t i", i=RUN),
+                )
+            return grouped
+
+        def quantise(grouped):
+            x_codes = quantised_pool.tile([P, PIXELS], U32, align_bytes=64)
+            x_scales = quantised_pool.tile([P, PIXELS], U8, align_bytes=64)
+            nc.vector.quantize_mx(
+                out=x_codes[:].bitcast(FP8X4), scales=x_scales[:], in_=grouped[:].rearrange("p w t -> p (w t)")
+            )
+            return x_codes, x_scales
+
+        def multiply(image, group, x_codes, x_scales):
+            for o_tile in range(O_TILES):
+                channels = slice(o_tile * P, (o_tile + 1) * P)
+                nc.tensor.matmul_mx(
+                    out=sums_of[(image, o_tile)][:],
+                    lhsT=w_words[:, group, channels].bitcast(FP8X4),
+                    lhsT_scale=w_scales[:, group, channels],
+                    rhs=x_codes[:].bitcast(FP8X4),
+                    rhs_scale=x_scales[:],
+                    start=(group == 0),
+                    stop=(group == GROUPS - 1),
+                )
+
+        def add_up(image, o_tile):
+            y = sums_of[(image, o_tile)]
+            nc.vector.tensor_reduce(
+                out=pooled[:, image, o_tile, 0:ROWS],
+                in_=y[:].rearrange("p (i j) -> p i j", j=COLS),
+                axis=AXIS_X,
+                op=ADD,
+            )
+            nc.vector.tensor_reduce(
+                out=pooled[:, image, o_tile, ROWS:POOLED],
+                in_=y[:].rearrange("p (i j) -> p j i", j=COLS),
+                axis=AXIS_X,
+                op=ADD,
+            )
+
+        def finish(image, o_tile):
+            for columns, count in ((slice(0, ROWS), COLS), (slice(ROWS, POOLED), ROWS)):
+                nc.scalar.activation(
+                    out=means[:, image, o_tile, columns],
+                    in_=pooled[:, image, o_tile, columns],
+                    func=IDENTITY,
+                    bias=bias[:, o_tile : o_tile + 1],
+                    scale=1.0 / count,
+                )
+
+        def store(image, o_tile):
+            nc.sync.dma_start(out=out_rows[o_tile][image], in_=means[:, image, o_tile, :])
+
+        grouped_of = {}
+        for step in range(CHUNKS + 1):
+            if step < CHUNKS:
+                image, group = divmod(step, GROUPS)
+                raw = load_x(image, group)
+                if step == 0:
+                    load_weight_scales()
+                    load_weight_words(0)
+                first_user = step + WEIGHT_LEAD
+                if WEIGHT_GROUPS <= first_user < GROUPS and first_user % WEIGHT_GROUPS == 0:
+                    load_weight_words(first_user)
+                grouped_of[step] = regroup(raw)
+            if step >= 1:
+                image, group = divmod(step - 1, GROUPS)
+                x_codes, x_scales = quantise(grouped_of[step - 1])
+                multiply(image, group, x_codes, x_scales)
+            if 0 <= step - (GROUPS + 1) < O_TILES:
+                add_up(0, step - (GROUPS + 1))
+            if 0 <= step - (GROUPS + 2) < O_TILES:
+                finish(0, step - (GROUPS + 2))
+        for o_tile in range(O_TILES):
+            store(0, o_tile)
+        for o_tile in range(O_TILES):
+            add_up(1, o_tile)
+            finish(1, o_tile)
+            store(1, o_tile)

@@ -29,6 +29,8 @@ POOLED = ROWS + COLS
 CHUNKS = IMAGES * GROUPS
 WEIGHT_GROUPS = 4
 WEIGHT_LEAD = 2
+LATE_TILE = 1
+IMAGE_0_ORDER = (0, 2, 3, LATE_TILE)
 RUN = 4
 VECTOR_PIXELS = 208
 
@@ -39,7 +41,8 @@ def tile_pam_module_pa_k_kernel(
     tc, x, Wq_words, Wq_scales, bq, Wk_words, Wk_scales, bk, Wv_words, Wv_scales, bv, out_0, out_1, out_2
 ):
     nc = tc.nc
-    weights = [(Wq_words, Wq_scales, 0), (Wk_words, Wk_scales, P), (Wv_words, Wv_scales, 2 * P)]
+    early_weights = [(Wq_words, Wq_scales, 0), (Wv_words, Wv_scales, 2 * P)]
+    late_weights = [(Wk_words, Wk_scales, LATE_TILE * P)]
     bias_rows = [bq, bk, bv[0:P], bv[P : 2 * P]]
     out_rows = [out_0, out_1, out_2[:, 0:P, :], out_2[:, P : 2 * P, :]]
 
@@ -47,7 +50,7 @@ def tile_pam_module_pa_k_kernel(
         keep = stack.enter_context(tc.tile_pool(name="keep", bufs=1))
         raw_pool = stack.enter_context(tc.tile_pool(name="raw", bufs=8))
         grouped_pool = stack.enter_context(tc.tile_pool(name="grouped", bufs=3))
-        quantised_pool = stack.enter_context(tc.tile_pool(name="quantised", bufs=6))
+        quantised_pool = stack.enter_context(tc.tile_pool(name="quantised", bufs=GROUPS + 2))
         psum = stack.enter_context(tc.psum_pool(name="psum", bufs=1))
         stack.enter_context(tc.manual_schedule())
 
@@ -71,7 +74,7 @@ def tile_pam_module_pa_k_kernel(
                 )
         nc.scalar.activation(out=bias[:], in_=bias_bf16[:, :, 0], func=IDENTITY)
 
-        def load_weight_scales():
+        def load_weight_scales(weights):
             for words, scales, first in weights:
                 n = scales.shape[2]
                 for quadrant in range(4):
@@ -80,7 +83,7 @@ def tile_pam_module_pa_k_kernel(
                         in_=scales[:, 4 * quadrant : 4 * quadrant + 4, :].rearrange("g q n -> q g n").bitcast(I32),
                     )
 
-        def load_weight_words(first_group):
+        def load_weight_words(weights, first_group):
             groups = slice(first_group, first_group + WEIGHT_GROUPS)
             for words, scales, first in weights:
                 n = words.shape[2]
@@ -117,8 +120,9 @@ def tile_pam_module_pa_k_kernel(
             )
             return x_codes, x_scales
 
-        def multiply(image, group, x_codes, x_scales):
-            for o_tile in range(O_TILES):
+        def multiply(image, group, o_tiles):
+            x_codes, x_scales = quantised_of[(image, group)]
+            for o_tile in o_tiles:
                 channels = slice(o_tile * P, (o_tile + 1) * P)
                 nc.tensor.matmul_mx(
                     out=sums_of[(image, o_tile)][:],
@@ -159,25 +163,35 @@ def tile_pam_module_pa_k_kernel(
             nc.sync.dma_start(out=out_rows[o_tile][image], in_=means[:, image, o_tile, :])
 
         grouped_of = {}
+        quantised_of = {}
         for step in range(CHUNKS + 1):
             if step < CHUNKS:
                 image, group = divmod(step, GROUPS)
+                late_groups = (step - GROUPS) * WEIGHT_GROUPS
+                if late_groups == 0:
+                    load_weight_scales(late_weights)
+                if 0 <= late_groups < GROUPS:
+                    load_weight_words(late_weights, late_groups)
                 raw = load_x(image, group)
                 if step == 0:
-                    load_weight_scales()
-                    load_weight_words(0)
+                    load_weight_scales(early_weights)
+                    load_weight_words(early_weights, 0)
                 first_user = step + WEIGHT_LEAD
                 if WEIGHT_GROUPS <= first_user < GROUPS and first_user % WEIGHT_GROUPS == 0:
-                    load_weight_words(first_user)
+                    load_weight_words(early_weights, first_user)
                 grouped_of[step] = regroup(raw)
             if step >= 1:
                 image, group = divmod(step - 1, GROUPS)
-                x_codes, x_scales = quantise(grouped_of[step - 1])
-                multiply(image, group, x_codes, x_scales)
+                quantised_of[(image, group)] = quantise(grouped_of[step - 1])
+                multiply(image, group, IMAGE_0_ORDER[0:3] if image == 0 else range(O_TILES))
+            late_groups = (step - GROUPS) * WEIGHT_GROUPS
+            if 0 <= late_groups < GROUPS:
+                for group in range(late_groups, late_groups + WEIGHT_GROUPS):
+                    multiply(0, group, [LATE_TILE])
             if 0 <= step - (GROUPS + 1) < O_TILES:
-                add_up(0, step - (GROUPS + 1))
+                add_up(0, IMAGE_0_ORDER[step - (GROUPS + 1)])
             if 0 <= step - (GROUPS + 2) < O_TILES:
-                finish(0, step - (GROUPS + 2))
+                finish(0, IMAGE_0_ORDER[step - (GROUPS + 2)])
         for o_tile in range(O_TILES):
             store(0, o_tile)
         for o_tile in range(O_TILES):

@@ -32,7 +32,8 @@ WEIGHT_LEAD = 2
 LATE_TILE = 1
 IMAGE_0_ORDER = (0, 2, 3, LATE_TILE)
 RUN = 4
-VECTOR_PIXELS = 208
+VECTOR_PIXELS = 232
+VECTOR_PIXELS_BESIDE_A_SUM = 136
 
 FLOPS = 2 * IMAGES * PIXELS * CHANNELS * OUT_CHANNELS
 
@@ -100,11 +101,11 @@ def tile_pam_module_pa_k_kernel(
             )
             return raw
 
-        def regroup(raw):
+        def regroup(raw, vector_pixels):
             grouped = grouped_pool.tile([P, PIXELS, PACK], BF16, align_bytes=64)
             for copy, pixels in (
-                (nc.vector.tensor_copy, slice(0, VECTOR_PIXELS)),
-                (nc.scalar.copy, slice(VECTOR_PIXELS, PIXELS)),
+                (nc.vector.tensor_copy, slice(0, vector_pixels)),
+                (nc.scalar.copy, slice(vector_pixels, PIXELS)),
             ):
                 copy(
                     out=grouped[:, pixels, :].rearrange("p (c i) t -> p c t i", i=RUN),
@@ -134,20 +135,22 @@ def tile_pam_module_pa_k_kernel(
                     stop=(group == GROUPS - 1),
                 )
 
-        def add_up(image, o_tile):
+        def add_up(image, o_tile, halves):
             y = sums_of[(image, o_tile)]
-            nc.vector.tensor_reduce(
-                out=pooled[:, image, o_tile, 0:ROWS],
-                in_=y[:].rearrange("p (i j) -> p i j", j=COLS),
-                axis=AXIS_X,
-                op=ADD,
-            )
-            nc.vector.tensor_reduce(
-                out=pooled[:, image, o_tile, ROWS:POOLED],
-                in_=y[:].rearrange("p (i j) -> p j i", j=COLS),
-                axis=AXIS_X,
-                op=ADD,
-            )
+            if 0 in halves:
+                nc.vector.tensor_reduce(
+                    out=pooled[:, image, o_tile, 0:ROWS],
+                    in_=y[:].rearrange("p (i j) -> p i j", j=COLS),
+                    axis=AXIS_X,
+                    op=ADD,
+                )
+            if 1 in halves:
+                nc.vector.tensor_reduce(
+                    out=pooled[:, image, o_tile, ROWS:POOLED],
+                    in_=y[:].rearrange("p (i j) -> p j i", j=COLS),
+                    axis=AXIS_X,
+                    op=ADD,
+                )
 
         def finish(image, o_tile):
             for columns, count in ((slice(0, ROWS), COLS), (slice(ROWS, POOLED), ROWS)):
@@ -179,7 +182,8 @@ def tile_pam_module_pa_k_kernel(
                 first_user = step + WEIGHT_LEAD
                 if WEIGHT_GROUPS <= first_user < GROUPS and first_user % WEIGHT_GROUPS == 0:
                     load_weight_words(early_weights, first_user)
-                grouped_of[step] = regroup(raw)
+                sums_here = 0 <= step - (GROUPS + 1) < 2 * O_TILES
+                grouped_of[step] = regroup(raw, VECTOR_PIXELS_BESIDE_A_SUM if sums_here else VECTOR_PIXELS)
             if step >= 1:
                 image, group = divmod(step - 1, GROUPS)
                 quantised_of[(image, group)] = quantise(grouped_of[step - 1])
@@ -188,13 +192,13 @@ def tile_pam_module_pa_k_kernel(
             if 0 <= late_groups < GROUPS:
                 for group in range(late_groups, late_groups + WEIGHT_GROUPS):
                     multiply(0, group, [LATE_TILE])
-            if 0 <= step - (GROUPS + 1) < O_TILES:
-                add_up(0, IMAGE_0_ORDER[step - (GROUPS + 1)])
-            if 0 <= step - (GROUPS + 2) < O_TILES:
-                finish(0, IMAGE_0_ORDER[step - (GROUPS + 2)])
+            if 0 <= step - (GROUPS + 1) < 2 * O_TILES:
+                add_up(0, IMAGE_0_ORDER[(step - (GROUPS + 1)) // 2], [(step - (GROUPS + 1)) % 2])
+            if 0 <= step - (GROUPS + 3) < 2 * O_TILES and (step - (GROUPS + 3)) % 2 == 0:
+                finish(0, IMAGE_0_ORDER[(step - (GROUPS + 3)) // 2])
         for o_tile in range(O_TILES):
             store(0, o_tile)
         for o_tile in range(O_TILES):
-            add_up(1, o_tile)
+            add_up(1, o_tile, [0, 1])
             finish(1, o_tile)
             store(1, o_tile)

@@ -27,13 +27,10 @@ O_TILES = OUT_CHANNELS // P
 POOLED = ROWS + COLS
 
 CHUNKS = IMAGES * GROUPS
-WEIGHT_GROUPS = 4
-WEIGHT_LEAD = 2
-LATE_TILE = 1
-IMAGE_0_ORDER = (0, 2, 3, LATE_TILE)
+LEAD = 4
 RUN = 4
 VECTOR_PIXELS = 232
-VECTOR_PIXELS_BESIDE_A_SUM = 136
+VECTOR_PIXELS_BESIDE_A_SUM = 80
 
 FLOPS = 2 * IMAGES * PIXELS * CHANNELS * OUT_CHANNELS
 
@@ -42,8 +39,7 @@ def tile_pam_module_pa_k_kernel(
     tc, x, Wq_words, Wq_scales, bq, Wk_words, Wk_scales, bk, Wv_words, Wv_scales, bv, out_0, out_1, out_2
 ):
     nc = tc.nc
-    early_weights = [(Wq_words, Wq_scales, 0), (Wv_words, Wv_scales, 2 * P)]
-    late_weights = [(Wk_words, Wk_scales, LATE_TILE * P)]
+    weights = [(Wq_words, Wq_scales, 0), (Wk_words, Wk_scales, P), (Wv_words, Wv_scales, 2 * P)]
     bias_rows = [bq, bk, bv[0:P], bv[P : 2 * P]]
     out_rows = [out_0, out_1, out_2[:, 0:P, :], out_2[:, P : 2 * P, :]]
 
@@ -51,7 +47,7 @@ def tile_pam_module_pa_k_kernel(
         keep = stack.enter_context(tc.tile_pool(name="keep", bufs=1))
         raw_pool = stack.enter_context(tc.tile_pool(name="raw", bufs=8))
         grouped_pool = stack.enter_context(tc.tile_pool(name="grouped", bufs=3))
-        quantised_pool = stack.enter_context(tc.tile_pool(name="quantised", bufs=GROUPS + 2))
+        quantised_pool = stack.enter_context(tc.tile_pool(name="quantised", bufs=4))
         psum = stack.enter_context(tc.psum_pool(name="psum", bufs=1))
         stack.enter_context(tc.manual_schedule())
 
@@ -75,22 +71,21 @@ def tile_pam_module_pa_k_kernel(
                 )
         nc.scalar.activation(out=bias[:], in_=bias_bf16[:, :, 0], func=IDENTITY)
 
-        def load_weight_scales(weights):
+        def load_weight_scales():
             for words, scales, first in weights:
                 n = scales.shape[2]
-                for quadrant in range(4):
+                for r in range(4):
                     nc.sync.dma_start(
-                        out=w_scales[32 * quadrant : 32 * quadrant + 4, :, first : first + n].bitcast(I32),
-                        in_=scales[:, 4 * quadrant : 4 * quadrant + 4, :].rearrange("g q n -> q g n").bitcast(I32),
+                        out=w_scales[r : P : 32, :, first : first + n].bitcast(I32),
+                        in_=scales[:, r : 16 : 4, :].rearrange("g q n -> q g n").bitcast(I32),
                     )
 
-        def load_weight_words(weights, first_group):
-            groups = slice(first_group, first_group + WEIGHT_GROUPS)
+        def load_weight_words(group):
             for words, scales, first in weights:
                 n = words.shape[2]
                 nc.sync.dma_start(
-                    out=w_words[:, groups, first : first + n].bitcast(I32),
-                    in_=words[groups].rearrange("g p n t -> p g (n t)").bitcast(I32),
+                    out=w_words[:, group, first : first + n].bitcast(I32),
+                    in_=words[group].rearrange("p n t -> p (n t)").bitcast(I32),
                 )
 
         def load_x(image, group):
@@ -121,9 +116,9 @@ def tile_pam_module_pa_k_kernel(
             )
             return x_codes, x_scales
 
-        def multiply(image, group, o_tiles):
+        def multiply(image, group):
             x_codes, x_scales = quantised_of[(image, group)]
-            for o_tile in o_tiles:
+            for o_tile in range(O_TILES):
                 channels = slice(o_tile * P, (o_tile + 1) * P)
                 nc.tensor.matmul_mx(
                     out=sums_of[(image, o_tile)][:],
@@ -165,38 +160,35 @@ def tile_pam_module_pa_k_kernel(
         def store(image, o_tile):
             nc.sync.dma_start(out=out_rows[o_tile][image], in_=means[:, image, o_tile, :])
 
+        chunks = [(0, group) for group in range(LEAD)]
+        for group in range(LEAD, GROUPS):
+            chunks.extend([(0, group), (1, group - LEAD)])
+        chunks.extend([(1, group) for group in range(GROUPS - LEAD, GROUPS)])
+        first_sum = chunks.index((0, GROUPS - 1)) + 2
+
         grouped_of = {}
         quantised_of = {}
         for step in range(CHUNKS + 1):
+            sums_here = 0 <= step - first_sum < O_TILES
             if step < CHUNKS:
-                image, group = divmod(step, GROUPS)
-                late_groups = (step - GROUPS) * WEIGHT_GROUPS
-                if late_groups == 0:
-                    load_weight_scales(late_weights)
-                if 0 <= late_groups < GROUPS:
-                    load_weight_words(late_weights, late_groups)
+                image, group = chunks[step]
                 raw = load_x(image, group)
                 if step == 0:
-                    load_weight_scales(early_weights)
-                    load_weight_words(early_weights, 0)
-                first_user = step + WEIGHT_LEAD
-                if WEIGHT_GROUPS <= first_user < GROUPS and first_user % WEIGHT_GROUPS == 0:
-                    load_weight_words(early_weights, first_user)
-                sums_here = 0 <= step - (GROUPS + 1) < 2 * O_TILES
+                    load_weight_scales()
+                if image == 0:
+                    load_weight_words(group)
                 grouped_of[step] = regroup(raw, VECTOR_PIXELS_BESIDE_A_SUM if sums_here else VECTOR_PIXELS)
             if step >= 1:
-                image, group = divmod(step - 1, GROUPS)
+                image, group = chunks[step - 1]
                 quantised_of[(image, group)] = quantise(grouped_of[step - 1])
-                multiply(image, group, IMAGE_0_ORDER[0:3] if image == 0 else range(O_TILES))
-            late_groups = (step - GROUPS) * WEIGHT_GROUPS
-            if 0 <= late_groups < GROUPS:
-                for group in range(late_groups, late_groups + WEIGHT_GROUPS):
-                    multiply(0, group, [LATE_TILE])
-            if 0 <= step - (GROUPS + 1) < 2 * O_TILES:
-                add_up(0, IMAGE_0_ORDER[(step - (GROUPS + 1)) // 2], [(step - (GROUPS + 1)) % 2])
-            if 0 <= step - (GROUPS + 3) < 2 * O_TILES and (step - (GROUPS + 3)) % 2 == 0:
-                finish(0, IMAGE_0_ORDER[(step - (GROUPS + 3)) // 2])
+                multiply(image, group)
+            if sums_here:
+                add_up(0, step - first_sum, [0, 1])
+            if 0 <= step - (first_sum + 1) < O_TILES:
+                finish(0, step - (first_sum + 1))
         for o_tile in range(O_TILES):
+            if first_sum + 1 + o_tile > CHUNKS:
+                finish(0, o_tile)
             store(0, o_tile)
         for o_tile in range(O_TILES):
             add_up(1, o_tile, [0, 1])

@@ -28,6 +28,7 @@ POOLED = ROWS + COLS
 
 CHUNKS = IMAGES * GROUPS
 LEAD = 4
+WEIGHT_GROUPS = 2
 RUN = 4
 VECTOR_PIXELS = 232
 VECTOR_PIXELS_BESIDE_A_SUM = 80
@@ -80,12 +81,13 @@ def tile_pam_module_pa_k_kernel(
                         in_=scales[:, r : 16 : 4, :].rearrange("g q n -> q g n").bitcast(I32),
                     )
 
-        def load_weight_words(group):
+        def load_weight_words(first_group):
+            groups = slice(first_group, first_group + WEIGHT_GROUPS)
             for words, scales, first in weights:
                 n = words.shape[2]
                 nc.sync.dma_start(
-                    out=w_words[:, group, first : first + n].bitcast(I32),
-                    in_=words[group].rearrange("p n t -> p (n t)").bitcast(I32),
+                    out=w_words[:, groups, first : first + n].bitcast(I32),
+                    in_=words[groups].rearrange("g p n t -> p g (n t)").bitcast(I32),
                 )
 
         def load_x(image, group):
@@ -175,7 +177,7 @@ def tile_pam_module_pa_k_kernel(
                 raw = load_x(image, group)
                 if step == 0:
                     load_weight_scales()
-                if image == 0:
+                if image == 0 and group % WEIGHT_GROUPS == 0:
                     load_weight_words(group)
                 grouped_of[step] = regroup(raw, VECTOR_PIXELS_BESIDE_A_SUM if sums_here else VECTOR_PIXELS)
             if step >= 1:

@@ -166,7 +166,7 @@ def tile_pam_module_pa_k_kernel(
         for group in range(LEAD, GROUPS):
             chunks.extend([(0, group), (1, group - LEAD)])
         chunks.extend([(1, group) for group in range(GROUPS - LEAD, GROUPS)])
-        first_sum = chunks.index((0, GROUPS - 1)) + 2
+        first_sum = chunks.index((0, GROUPS - 1)) + 3
 
         grouped_of = {}
         quantised_of = {}

@@ -186,11 +186,8 @@ def tile_pam_module_pa_k_kernel(
                 multiply(image, group)
             if sums_here:
                 add_up(0, step - first_sum, [0, 1])
-            if 0 <= step - (first_sum + 1) < O_TILES:
-                finish(0, step - (first_sum + 1))
         for o_tile in range(O_TILES):
-            if first_sum + 1 + o_tile > CHUNKS:
-                finish(0, o_tile)
+            finish(0, o_tile)
             store(0, o_tile)
         for o_tile in range(O_TILES):
             add_up(1, o_tile, [0, 1])

from contextlib import ExitStack

import concourse.mybir as mybir

F32 = mybir.dt.float32
BF16 = mybir.dt.bfloat16
I32 = mybir.dt.int32
U32 = mybir.dt.uint32
U8 = mybir.dt.uint8
FP8X4 = mybir.dt.float8_e4m3fn_x4
ADD = mybir.AluOpType.add
AXIS_X = mybir.AxisListType.X
IDENTITY = mybir.ActivationFunctionType.Identity

P = 128
PACK = 4
K_PASS = P * PACK

IMAGES = 2
CHANNELS = 8192
ROWS = 16
COLS = 32
PIXELS = ROWS * COLS
GROUPS = CHANNELS // K_PASS
OUT_CHANNELS = 512
O_TILES = OUT_CHANNELS // P
POOLED = ROWS + COLS

CHUNKS = IMAGES * GROUPS
LEAD = 4
WEIGHT_GROUPS = 2
RUN = 4
VECTOR_PIXELS = 232
VECTOR_PIXELS_BESIDE_A_SUM = 80

FLOPS = 2 * IMAGES * PIXELS * CHANNELS * OUT_CHANNELS


def tile_pam_module_pa_k_kernel(
    tc, x, Wq_words, Wq_scales, bq, Wk_words, Wk_scales, bk, Wv_words, Wv_scales, bv, out_0, out_1, out_2
):
    nc = tc.nc
    weights = [(Wq_words, Wq_scales, 0), (Wk_words, Wk_scales, P), (Wv_words, Wv_scales, 2 * P)]
    bias_rows = [bq, bk, bv[0:P], bv[P : 2 * P]]
    out_rows = [out_0, out_1, out_2[:, 0:P, :], out_2[:, P : 2 * P, :]]

    with ExitStack() as stack:
        keep = stack.enter_context(tc.tile_pool(name="keep", bufs=1))
        raw_pool = stack.enter_context(tc.tile_pool(name="raw", bufs=8))
        grouped_pool = stack.enter_context(tc.tile_pool(name="grouped", bufs=3))
        quantised_pool = stack.enter_context(tc.tile_pool(name="quantised", bufs=4))
        psum = stack.enter_context(tc.psum_pool(name="psum", bufs=1))
        stack.enter_context(tc.manual_schedule())

        w_words = keep.tile([P, GROUPS, OUT_CHANNELS], U32, align_bytes=64)
        w_scales = keep.tile([P, GROUPS, OUT_CHANNELS], U8, align_bytes=64)
        bias_bf16 = keep.tile([P, O_TILES, 16], BF16)
        bias = keep.tile([P, O_TILES], F32)
        pooled = keep.tile([P, IMAGES, O_TILES, POOLED], F32)
        means = keep.tile([P, IMAGES, O_TILES, POOLED], F32)
        sums_of = {}
        for image in range(IMAGES):
            for o_tile in range(O_TILES):
                sums_of[(image, o_tile)] = psum.tile([P, PIXELS], F32, name="y_%d_%d" % (image, o_tile))

        nc.vector.memset(w_scales[:].rearrange("p g n -> p (g n)").bitcast(I32), 0)

        with nc.allow_non_contiguous_dma(reason="128 bias values, one to a partition"):
            for o_tile in range(O_TILES):
                nc.scalar.dma_start(
                    out=bias_bf16[:, o_tile, 0:1], in_=bias_rows[o_tile].rearrange("(o u) -> o u", u=1)
                )
        nc.scalar.activation(out=bias[:], in_=bias_bf16[:, :, 0], func=IDENTITY)

        def load_weight_scales():
            for words, scales, first in weights:
                n = scales.shape[2]
                for r in range(4):
                    nc.sync.dma_start(
                        out=w_scales[r : P : 32, :, first : first + n].bitcast(I32),
                        in_=scales[:, r : 16 : 4, :].rearrange("g q n -> q g n").bitcast(I32),
                    )

        def load_weight_words(first_group):
            groups = slice(first_group, first_group + WEIGHT_GROUPS)
            for words, scales, first in weights:
                n = words.shape[2]
                nc.sync.dma_start(
                    out=w_words[:, groups, first : first + n].bitcast(I32),
                    in_=words[groups].rearrange("g p n t -> p g (n t)").bitcast(I32),
                )

        def load_x(image, group):
            raw = raw_pool.tile([P, PACK, PIXELS], BF16)
            nc.sync.dma_start(
                out=raw[:],
                in_=x[image, group * K_PASS : (group + 1) * K_PASS].rearrange("(p t) h w -> p t (h w)", t=PACK),
            )
            return raw

        def regroup(raw, vector_pixels):
            grouped = grouped_pool.tile([P, PIXELS, PACK], BF16, align_bytes=64)
            for copy, pixels in (
                (nc.vector.tensor_copy, slice(0, vector_pixels)),
                (nc.scalar.copy, slice(vector_pixels, PIXELS)),
            ):
                copy(
                    out=grouped[:, pixels, :].rearrange("p (c i) t -> p c t i", i=RUN),
                    in_=raw[:, :, pixels].rearrange("p t (c i) -> p c t i", i=RUN),
                )
            return grouped

        def quantise(grouped):
            x_codes = quantised_pool.tile([P, PIXELS], U32, align_bytes=64)
            x_scales = quantised_pool.tile([P, PIXELS], U8, align_bytes=64)
            nc.vector.quantize_mx(
                out=x_codes[:].bitcast(FP8X4), scales=x_scales[:], in_=grouped[:].rearrange("p w t -> p (w t)")
            )
            return x_codes, x_scales

        def multiply(image, group):
            x_codes, x_scales = quantised_of[(image, group)]
            for o_tile in range(O_TILES):
                channels = slice(o_tile * P, (o_tile + 1) * P)
                nc.tensor.matmul_mx(
                    out=sums_of[(image, o_tile)][:],
                    lhsT=w_words[:, group, channels].bitcast(FP8X4),
                    lhsT_scale=w_scales[:, group, channels],
                    rhs=x_codes[:].bitcast(FP8X4),
                    rhs_scale=x_scales[:],
                    start=(group == 0),
                    stop=(group == GROUPS - 1),
                )

        def add_up(image, o_tile, halves):
            y = sums_of[(image, o_tile)]
            if 0 in halves:
                nc.vector.tensor_reduce(
                    out=pooled[:, image, o_tile, 0:ROWS],
                    in_=y[:].rearrange("p (i j) -> p i j", j=COLS),
                    axis=AXIS_X,
                    op=ADD,
                )
            if 1 in halves:
                nc.vector.tensor_reduce(
                    out=pooled[:, image, o_tile, ROWS:POOLED],
                    in_=y[:].rearrange("p (i j) -> p j i", j=COLS),
                    axis=AXIS_X,
                    op=ADD,
                )

        def finish(image, o_tile):
            for columns, count in ((slice(0, ROWS), COLS), (slice(ROWS, POOLED), ROWS)):
                nc.scalar.activation(
                    out=means[:, image, o_tile, columns],
                    in_=pooled[:, image, o_tile, columns],
                    func=IDENTITY,
                    bias=bias[:, o_tile : o_tile + 1],
                    scale=1.0 / count,
                )

        def store(image, o_tile):
            nc.sync.dma_start(out=out_rows[o_tile][image], in_=means[:, image, o_tile, :])

        chunks = [(0, group) for group in range(LEAD)]
        for group in range(LEAD, GROUPS):
            chunks.extend([(0, group), (1, group - LEAD)])
        chunks.extend([(1, group) for group in range(GROUPS - LEAD, GROUPS)])
        first_sum = chunks.index((0, GROUPS - 1)) + 3

        grouped_of = {}
        quantised_of = {}
        for step in range(CHUNKS + 1):
            sums_here = 0 <= step - first_sum < O_TILES
            if step < CHUNKS:
                image, group = chunks[step]
                raw = load_x(image, group)
                if step == 0:
                    load_weight_scales()
                if image == 0 and group % WEIGHT_GROUPS == 0:
                    load_weight_words(group)
                grouped_of[step] = regroup(raw, VECTOR_PIXELS_BESIDE_A_SUM if sums_here else VECTOR_PIXELS)
            if step >= 1:
                image, group = chunks[step - 1]
                quantised_of[(image, group)] = quantise(grouped_of[step - 1])
                multiply(image, group)
            if sums_here:
                add_up(0, step - first_sum, [0, 1])
        for o_tile in range(O_TILES):
            finish(0, o_tile)
            store(0, o_tile)
        for o_tile in range(O_TILES):
            add_up(1, o_tile, [0, 1])
            finish(1, o_tile)
            store(1, o_tile)
